import numpy as np
import ml_dtypes


def mxq(x, axis, fmt="e4m3"):
    dtype, down = {"e4m3": (ml_dtypes.float8_e4m3fn, 7), "e5m2": (ml_dtypes.float8_e5m2, 14)}[fmt]
    v = np.moveaxis(np.asarray(x, np.float32).astype(ml_dtypes.bfloat16).astype(np.float64), axis, -1)
    blocks = v.reshape(v.shape[:-1] + (-1, 32))
    amax = np.abs(blocks).max(-1, keepdims=True)
    byte = np.maximum(np.where(amax > 0, np.frexp(amax)[1] - 1 + 127, 0) - down, 1)
    scale = np.exp2(byte - 127.0)
    codes = (blocks / scale).astype(np.float32).astype(dtype).astype(np.float64)
    return np.moveaxis((codes * scale).reshape(v.shape), -1, axis)


WIDE = False


def mx_kscale(k):
    if not WIDE:
        return np.ones(k)
    levels = np.array([18, -18])
    if k % 512:
        return np.exp2(np.random.permutation(np.resize(levels, k // 32))).repeat(32)
    a = np.empty((k // 512, 16))
    for p in range(k // 512):
        a[p, :8] = np.random.permutation(np.resize(levels, 8))
        for g in range(8):
            far = levels[np.abs(levels - a[p, g]) >= 10]
            a[p, g + 8] = far[np.random.randint(len(far))]
    return np.exp2(a.ravel()).repeat(32)


BF16 = ml_dtypes.bfloat16


def bf(x):
    return np.asarray(x, np.float32).astype(BF16)


def f64(x):
    return np.asarray(x).astype(np.float64)


B, S, H, HD = 1, 1024, 2, 512
D = H * HD


def sigmoid(x):
    e = np.exp(-np.abs(x))
    return np.where(x >= 0.0, 1.0, e) / (1.0 + e)


def split_heads(x):
    return x.reshape(B, S, H, HD).transpose(0, 2, 1, 3)


def merge_heads(x):
    return x.transpose(0, 2, 1, 3).reshape(B, S, D)


def setup_inputs():
    s = mx_kscale(S)[None, :, None]
    u = np.tile(mx_kscale(HD), H)[None, None, :]
    c = mx_kscale(S)[None, :, None]
    v0 = bf(np.random.standard_normal((B, S, D)) * 4.0 / np.sqrt(S))
    k0 = bf(np.random.standard_normal((B, S, D)) * 1.2 / HD ** 0.25)
    q0 = bf(np.random.standard_normal((B, S, D)) * 1.2 / HD ** 0.25)
    g = bf(np.random.standard_normal((B, S, D)) * np.exp2(np.random.randint(-6, 1, (B, S, 1))) / s * u)
    scores = split_heads(f64(q0)) @ split_heads(f64(k0)).transpose(0, 1, 3, 2)
    return {"v": bf(f64(v0) * c / u),
            "k": bf(f64(k0) / c),
            "q": bf(f64(q0) * s),
            "scores": np.asarray(scores, np.float32),
            "grad_out": g}


def reference(v, k, q, scores, grad_out):
    vh = split_heads(f64(v))
    kh = split_heads(f64(k))
    qh = split_heads(f64(q))
    gh = split_heads(f64(grad_out))
    z = f64(scores)
    sg = sigmoid(z)
    dp = mxq(gh, 3, "e5m2") @ mxq(vh, 3, "e4m3").transpose(0, 1, 3, 2)
    ds = dp * (sg * (1.0 + z * (1.0 - sg)))
    dq = mxq(ds, 3, "e5m2") @ mxq(kh, 2, "e4m3")
    dk = mxq(ds, 2, "e5m2").transpose(0, 1, 3, 2) @ mxq(qh, 2, "e4m3")
    return merge_heads(dq), merge_heads(dk)

from contextlib import ExitStack

import concourse.mybir as mybir
from concourse.masks import make_identity

SEQ, HEADS, HD = 1024, 2, 512
P = 128
PACK = 4
PASS = P * PACK

FLOPS = 3 * 2 * HEADS * SEQ * SEQ * HD

F32 = mybir.dt.float32
BF16 = mybir.dt.bfloat16
U32 = mybir.dt.uint32
U8 = mybir.dt.uint8
E4M3 = mybir.dt.float8_e4m3fn_x4
E5M2 = mybir.dt.float8_e5m2_x4
ADD, SUB, MULT = mybir.AluOpType.add, mybir.AluOpType.subtract, mybir.AluOpType.mult
ACT = mybir.ActivationFunctionType

BLOCKS = 8

ACTS = ([("silu", b) for b in (0,)] + [("sig", b) for b in (0, 1,)] + [("silu", b) for b in (1, 2, 3,)] + [("sig", b) for b in (2, 3, 4, 5,)] + [("silu", b) for b in (4, 5, 6, 7,)] + [("sig", b) for b in (6, 7,)])
LEAD = 5
FIRST_BUFS = 4


def tile_pointwisespaggregatedattention_v_kernel(tc, v, k, q, scores, grad_out, out_0, out_1):
    nc = tc.nc
    with ExitStack() as ctx:
        const = ctx.enter_context(tc.tile_pool(name="const", bufs=1))
        raws = ctx.enter_context(tc.tile_pool(name="raws", bufs=2))
        stage = ctx.enter_context(tc.tile_pool(name="stage", bufs=2))
        big = ctx.enter_context(tc.tile_pool(name="big", bufs=3))
        codes = ctx.enter_context(tc.tile_pool(name="codes", bufs=2))
        outs = ctx.enter_context(tc.tile_pool(name="outs", bufs=8))
        psum_dp = ctx.enter_context(tc.psum_pool(name="psum_dp", bufs=3))
        psum_tr = ctx.enter_context(tc.psum_pool(name="psum_tr", bufs=2))
        psum_acc = ctx.enter_context(tc.psum_pool(name="psum_acc", bufs=3))

        ident = const.tile([P, P], F32)
        make_identity(nc, ident[:])
        ctx.enter_context(tc.manual_schedule())
        warm = const.tile([P, 1], F32)
        nc.vector.memset(warm[:], 0.0)
        nc.scalar.activation(out=warm[:], in_=warm[:], func=ACT.Silu)

        raw, z, first, ds, a_in, b_in = {}, {}, {}, {}, {}, {}
        v_codes, g_codes, k_codes, q_codes, a_codes, b_codes = {}, {}, {}, {}, {}, {}
        dp_bank, tr_bank, grouped = {}, {}, {}

        def head_rows(x, h, r):
            return x[0, r * PASS : (r + 1) * PASS, h * HD : (h + 1) * HD]

        def load(name, x, h, r, parts=1):
            t = raws.tile([P, PACK, HD], BF16, name="raw_" + name)
            view = "(j p) w -> p j w" if name == "v" else "(p j) w -> p j w"
            src = head_rows(x, h, r).rearrange(view, j=PACK)
            for j in range(0, PACK, PACK // parts):
                nc.sync.dma_start(out=t[:, j : j + PACK // parts], in_=src[:, j : j + PACK // parts])
            raw[name, h, r] = t

        def load_scores(h, r, j0, j1, c0, c1):
            if (h, r) not in z:
                z[h, r] = big.tile([P, PACK, SEQ], F32, name="z")
            rows = scores[0, h, r * PASS : (r + 1) * PASS, :].rearrange("(p j) c -> p j c", j=PACK)
            nc.sync.dma_start(out=z[h, r][:, j0:j1, c0:c1], in_=rows[:, j0:j1, c0:c1])

        def quantize(dest, col, kind, src):
            words, scales = dest
            n = src.shape[1] // PACK
            nc.vector.quantize_mx(
                out=words[:, col : col + n].bitcast(kind), scales=scales[:, col : col + n], in_=src
            )

        def code_tile(name, cols, bufs):
            words = codes.tile([P, cols], U32, align_bytes=64, name=name + "_w", bufs=bufs)
            scales = codes.tile([P, cols], U8, align_bytes=64, name=name + "_s", bufs=bufs)
            return words, scales

        def turn(src, pair):
            bank = psum_tr.tile([P, 2, 2, P], F32, name="tr")
            words = src[:].bitcast(F32)
            half = words.shape[2]
            for a in range(2):
                for u in range(2):
                    nc.tensor.transpose(bank[:, a, u, :], words[:, 2 * pair + a, u:half:2], ident[:])
            return bank

        def group(engine, bank, dest, pair):
            o = dest[:].rearrange("p c j -> p (c j)").bitcast(F32).rearrange("p (a r u) -> p a r u", a=PACK, u=2)
            o = o[:, 2 * pair : 2 * pair + 2]
            i = bank[:].rearrange("p a u r -> p a r u")
            if engine == "v":
                nc.vector.tensor_copy(out=o, in_=i)
            else:
                nc.scalar.copy(out=o, in_=i)

        def flat(t):
            return t[:].rearrange("p c j -> p (c j)")

        def turn_input(name, h, r, pair):
            return turn(raw[name, h, r], pair)

        def group_turned(name, h, r, pair, bank, engine):
            if pair == 0:
                grouped[name, h, r] = stage.tile([P, PASS, PACK], BF16, align_bytes=64, name="turned")
            group(engine, bank, grouped[name, h, r], pair)

        def quant_turned(name, h, r):
            store = v_codes if name == "v" else g_codes
            if name == "v":
                if r == 0:
                    store[h] = code_tile("v", SEQ, 2)
                quantize(store[h], r * PASS, E4M3, flat(grouped[name, h, r]))
            else:
                store[h, r] = code_tile("g", PASS, 2)
                quantize(store[h, r], 0, E5M2, flat(grouped[name, h, r]))

        def interleave(dest, src, c0, c1):
            nc.vector.tensor_copy(
                out=dest[:, c0:c1, :].rearrange("p (c i) j -> p c j i", i=4),
                in_=src[:, :, c0:c1].rearrange("p j (c i) -> p c j i", i=4),
            )

        def group_input(name, h, r, engine="v"):
            t = stage.tile([P, PASS, PACK], BF16, align_bytes=64, name="grouped")
            if engine == "v":
                interleave(t, raw[name, h, r], 0, HD)
            else:
                for s in range(2):
                    cs = slice(s * HD // 2, (s + 1) * HD // 2)
                    nc.scalar.copy(out=t[:, cs, :], in_=raw[name, h, r][:, :, cs].rearrange("p j c -> p c j"))
            grouped[name, h, r] = t

        def quant_grouped(name, h, r):
            store = k_codes if name == "k" else q_codes
            store[h, r] = code_tile(name, HD, 4)
            quantize(store[h, r], 0, E4M3, flat(grouped[name, h, r]))

        def where(b):
            return b // 4, b // 2 % 2, b % 2

        def factor(kind, b):
            for a, kk in ACTS:
                if kk == b:
                    return a == kind
            return False

        def activate(index):
            kind, b = ACTS[index // 2]
            js = slice(index % 2 * 2, index % 2 * 2 + 2)
            h, r, c = where(b)
            src = z[h, r][:, js, c * PASS : (c + 1) * PASS]
            if factor(kind, b):
                if b not in first:
                    first[b] = big.tile([P, PACK, PASS], F32, name="first", bufs=FIRST_BUFS)
                dst = first[b][:, js, :]
            else:
                dst = src
            if kind == "silu":
                nc.scalar.activation(out=dst, in_=src, func=ACT.Silu, scale=-1.0)
            else:
                nc.scalar.activation(out=dst, in_=src, func=ACT.Sigmoid)

        def product(n):
            b, j = n // 4, n % 4
            h, r, c = where(b)
            bank = psum_dp.tile([P, PASS], F32, name="dp")
            gw, gs = g_codes[h, r]
            vw, vs = v_codes[h]
            cols = slice(c * PASS, (c + 1) * PASS)
            rows = slice(j * P, (j + 1) * P)
            nc.tensor.matmul_mx(
                out=bank[:],
                lhsT=gw[:, rows].bitcast(E5M2),
                lhsT_scale=gs[:, rows],
                rhs=vw[:, cols].bitcast(E4M3),
                rhs_scale=vs[:, cols],
                start=True,
                stop=True,
            )
            dp_bank[n] = bank

        def times_first(n):
            b, j = n // 4, n % 4
            f = first[b][:, j, :]
            if factor("silu", b):
                nc.vector.scalar_tensor_tensor(out=f, in0=f, scalar=1.0, in1=dp_bank[n][:], op0=SUB, op1=MULT)
            else:
                nc.vector.scalar_tensor_tensor(out=f, in0=dp_bank[n][:], scalar=-1.0, in1=f, op0=MULT, op1=MULT)

        def times_second(n):
            b, j = n // 4, n % 4
            h, r, c = where(b)
            if j == 0:
                ds[b] = stage.tile([P, PACK, PASS], BF16, align_bytes=64, name="ds")
            f = first[b][:, j, :]
            s = z[h, r][:, j, c * PASS : (c + 1) * PASS]
            if factor("silu", b):
                nc.vector.scalar_tensor_tensor(out=ds[b][:, j, :], in0=f, scalar=-1.0, in1=s, op0=MULT, op1=MULT)
            else:
                nc.vector.scalar_tensor_tensor(out=ds[b][:, j, :], in0=s, scalar=1.0, in1=f, op0=SUB, op1=MULT)

        def turn_ds(b, pair):
            return turn(ds[b], pair)

        def group_a(b, pair, bank, engine):
            if pair == 0:
                a_in[b] = stage.tile([P, PASS, PACK], BF16, align_bytes=64, name="a_in")
            group(engine, bank, a_in[b], pair)

        def quant_a(b, pair):
            if pair == 0:
                a_codes[b] = code_tile("a", PASS, 4)
            half = PASS * PACK // 2
            quantize(a_codes[b], pair * PASS // 2, E5M2, flat(a_in[b])[:, pair * half : (pair + 1) * half])

        def group_b(b, c0, c1):
            if c0 == 0:
                b_in[b] = stage.tile([P, PASS, PACK], BF16, align_bytes=64, name="b_in")
            interleave(b_in[b], ds[b], c0, c1)

        def quant_b(b, c0, c1):
            if c0 == 0:
                b_codes[b] = code_tile("b", PASS, 6)
            quantize(b_codes[b], c0, E5M2, flat(b_in[b])[:, PACK * c0 : PACK * c1])

        def result(lhs, rhs, j, dest, spare=False):
            acc = psum_dp.tile([P, PASS], F32, name="dp") if spare else psum_acc.tile([P, HD], F32, name="acc")
            for i in range(2):
                (lw, ls), (rw, rs) = lhs[i], rhs[i]
                nc.tensor.matmul_mx(
                    out=acc[:],
                    lhsT=lw[:, j * P : (j + 1) * P].bitcast(E5M2),
                    lhsT_scale=ls[:, j * P : (j + 1) * P],
                    rhs=rw[:].bitcast(E4M3),
                    rhs_scale=rs[:],
                    start=(i == 0),
                    stop=(i == 1),
                )
            return acc, dest

        def store(pending, engine):
            acc, dest = pending
            t = outs.tile([P, HD], F32, name="result")
            if engine == "v":
                nc.vector.tensor_copy(out=t[:], in_=acc[:])
            else:
                nc.scalar.copy(out=t[:], in_=acc[:])
            nc.sync.dma_start(out=dest, in_=t[:])

        def dq_tile(h, r, j, spare=False):
            rows = head_rows(out_0, h, r).rearrange("(m j) w -> j m w", j=PACK)
            return result([a_codes[4 * h + 2 * r + c] for c in range(2)], [k_codes[h, c] for c in range(2)], j, rows[j], spare)

        def dk_tile(h, c, j, spare=False):
            rows = head_rows(out_1, h, c)
            return result([b_codes[4 * h + 2 * r + c] for r in range(2)], [q_codes[h, r] for r in range(2)], j, rows[j * P : (j + 1) * P], spare)

        plan = {}

        def at(n, rank, fn):
            plan.setdefault(n, []).append((rank, len(plan.get(n, [])), fn))

        box = {}

        LOADS = [(-9, ("g", 0, 0)), (-9, ("v", 0, 0)), (-9, ("z", 0, 0, 0, 2, 0, 512)), (-9, ("z", 0, 0, 2, 4, 0, 512)), (-9, ("v", 0, 1)), (-9, ("k", 0, 0)), (-9, ("z", 0, 0, 0, 4, 512, 1024)), (-9, ("k", 0, 1)), (-9, ("g", 0, 1)), (-9, ("z", 0, 1, 0, 2, 0, 1024)), (-9, ("z", 0, 1, 2, 4, 0, 1024)), (-9, ("q", 0, 0)), (-9, ("q", 0, 1)), (-3, ("z", 1, 0, 0, 2, 0, 1024)), (-3, ("v", 1, 0)), (-3, ("z", 1, 0, 2, 4, 0, 1024)), (-3, ("g", 1, 0)), (2, ("v", 1, 1)), (3, ("k", 1, 0)), (6, ("g", 1, 1)), (7, ("k", 1, 1)), (9, ("z", 1, 1, 0, 2, 0, 1024)), (9, ("z", 1, 1, 2, 4, 0, 1024)), (10, ("q", 1, 0)), (11, ("q", 1, 1))]
        def do_load(spec):
            if spec[0] == "z":
                load_scores(*spec[1:])
            else:
                load(spec[0], {"v": v, "k": k, "q": q, "g": grad_out}[spec[0]], *spec[1:])

        for n, spec in LOADS:
            at(n, 0, lambda spec=spec: do_load(spec))

        for i in range(2 * len(ACTS)):
            at(i - LEAD, 2, lambda i=i: activate(i))
        for n in range(4 * BLOCKS):
            at(n - 2, 3, lambda n=n: product(n))
            at(n, 4, lambda n=n: times_first(n))
            at(n + 1, 4.5, lambda n=n: times_second(n))

        def turned(n, name, h, r, engines, lag=1):
            for pair in range(2):
                key = (name, h, r, pair)
                def go(pair=pair, key=key):
                    box[key] = turn_input(name, h, r, pair)
                def cp(pair=pair, key=key):
                    group_turned(name, h, r, pair, box[key], engines[pair])
                at(n + pair * 1, 5.5, go)
                at(n + pair * 1 + lag, 1 if engines[pair] == "s" else 6, cp)
            at(n + 1 + lag + (1 if engines[1] == "s" else 0), 6.1, lambda: quant_turned(name, h, r))

        def interleaved(n, name, h, r, engine="v"):
            at(n, 6 if engine == "v" else 2.5, lambda: group_input(name, h, r, engine))
            at(n + 1, 6, lambda: quant_grouped(name, h, r))

        turned(-8, "g", 0, 0, "vv")
        turned(-6, "v", 0, 0, "vv")
        turned(-2, "v", 0, 1, "vv")
        interleaved(1, "k", 0, 0)
        turned(2, "g", 0, 1, "ss")
        interleaved(4, "k", 0, 1)
        interleaved(7, "q", 0, 0)
        interleaved(9, "q", 0, 1)
        turned(10, "v", 1, 0, "ss")
        turned(9, "g", 1, 0, "ss")
        turned(14, "v", 1, 1, "ss")
        interleaved(16, "k", 1, 0)
        interleaved(18, "k", 1, 1)
        turned(18, "g", 1, 1, "ss")
        interleaved(20, "q", 1, 0)
        interleaved(22, "q", 1, 1)

        def block(b, fast):
            n0 = 4 * b
            h, r, c = where(b)
            for pair in range(2):
                def go(pair=pair):
                    box["a", b, pair] = turn_ds(b, pair)
                def cp(pair=pair):
                    group_a(b, pair, box["a", b, pair], "s")
                n = n0 + 2 * pair + (2 if fast else 3)
                at(n, 5, go)
                at(n + (0 if fast else 1), 5.2 if fast else 1, cp)
                at(n + (1 if fast else 2), 6.2, lambda pair=pair: quant_a(b, pair))
            if fast:
                for s in range(2):
                    at(n0 + 4, 6, lambda s=s: group_b(b, s * PASS // 2, (s + 1) * PASS // 2))
                for s in range(2):
                    at(n0 + 5, 6, lambda s=s: quant_b(b, s * PASS // 2, (s + 1) * PASS // 2))
            else:
                at(n0 + 5, 6, lambda: group_b(b, 0, PASS))
                at(n0 + 5 + 1, 6, lambda: quant_b(b, 0, PASS))

        for b in range(BLOCKS):
            block(b, b == BLOCKS - 1)

        def results(n, b, what, per, engines, lag=1, js=range(4), spare=False, rank=7):
            h, r, c = where(b)
            for i, j in enumerate(js):
                def go(j=j):
                    box[what, b, j] = dq_tile(h, r, j, spare) if what == "dq" else dk_tile(h, c, j, spare)
                m = n + i // per
                at(m, rank + 0.1 * i, go)
                e = engines[i]
                at(m + lag, (1 if e == "s" else 6.5) if lag else rank + 0.1 * i + 0.25, lambda j=j, e=e: store(box[what, b, j], e))

        results(10, 1, "dq", 1, "ssss")
        results(15, 2, "dk", 1, "ssss")
        results(19, 3, "dq", 2, "ssss")
        results(21, 3, "dk", 2, "ssss")
        results(26, 5, "dq", 2, "ssss")
        results(30, 6, "dk", 2, "svsv")
        results(32, 7, "dq", 2, "ss", lag=1, js=(0,1))
        results(33, 7, "dk", 4, "svsv", lag=0, spare=True)
        results(34, 7, "dq", 2, "sv", lag=0, js=(2,3))

        for n in sorted(plan):
            for rank, i, fn in sorted(plan[n], key=lambda x: x[:2]):
                fn()
